import numpy as np
import ml_dtypes


def mxq(x, axis, fmt="e4m3"):
    dtype, down = {"e4m3": (ml_dtypes.float8_e4m3fn, 7), "e5m2": (ml_dtypes.float8_e5m2, 14)}[fmt]
    v = np.moveaxis(np.asarray(x, np.float32).astype(ml_dtypes.bfloat16).astype(np.float64), axis, -1)
    blocks = v.reshape(v.shape[:-1] + (-1, 32))
    amax = np.abs(blocks).max(-1, keepdims=True)
    byte = np.maximum(np.where(amax > 0, np.frexp(amax)[1] - 1 + 127, 0) - down, 1)
    scale = np.exp2(byte - 127.0)
    codes = (blocks / scale).astype(np.float32).astype(dtype).astype(np.float64)
    return np.moveaxis((codes * scale).reshape(v.shape), -1, axis)


WIDE = False


def mx_kscale(k):
    if not WIDE:
        return np.ones(k)
    levels = np.array([10, -10, 5, -5, 0])
    a = np.random.permutation(np.resize(levels, k // 512 * 4)).reshape(k // 512, 4)
    idx = np.arange(k)
    return np.exp2(a[idx // 512, idx % 128 // 32])


BF16 = ml_dtypes.bfloat16


def bf(x):
    return np.asarray(x, np.float32).astype(BF16)


def f64(x):
    return np.asarray(x).astype(np.float64)


B, N, HID, L, R, KS = 4, 2048, 1024, 1, 1, 64
H = R * L
OUT = 2 * H * KS
HALF = KS // 2


def mass_sincos(node_mass):
    inv_freq = np.exp(-np.log(10000.0) * np.arange(HALF) / HALF)
    ang = node_mass[..., None, None] * inv_freq
    return np.sin(ang), np.cos(ang)


def setup_inputs():
    s = mx_kscale(HID)
    return {"node": bf(np.random.standard_normal((B, N, HID)) * s),
            "node_mass": bf(np.random.random((B, N)) * 10.0),
            "W": bf(np.random.standard_normal((HID, OUT)) / np.sqrt(HID) / s[:, None]),
            "b": bf(np.random.standard_normal(OUT) * 0.3)}


def reference(node, node_mass, W, b):
    kv = ((mxq(f64(node), 2, "e4m3") @ mxq(f64(W), 0, "e4m3")) + f64(b)).reshape(B, N, 2 * H, KS)
    k_cache, v_cache = kv[:, :, :H, :], kv[:, :, H:, :]
    dis_sin, dis_cos = mass_sincos(f64(node_mass))
    x0, x1 = k_cache[..., :HALF], k_cache[..., HALF:]
    k_cache = np.concatenate([x0 * dis_cos - x1 * dis_sin, x0 * dis_sin + x1 * dis_cos], axis=-1)
    k_out = np.swapaxes(k_cache, 1, 2)
    v_out = np.swapaxes(v_cache, 1, 2)
    return np.stack([k_out, v_out], axis=0)

@@ -1,0 +1,268 @@
+import math
+from contextlib import ExitStack
+
+import concourse.mybir as mybir
+from concourse.masks import make_identity
+
+FLOPS = 2 * 8192 * 1024 * 128
+
+F32 = mybir.dt.float32
+BF16 = mybir.dt.bfloat16
+I32 = mybir.dt.int32
+U32 = mybir.dt.uint32
+U8 = mybir.dt.uint8
+FP8X4 = mybir.dt.float8_e4m3fn_x4
+ALU = mybir.AluOpType
+ACT = mybir.ActivationFunctionType
+
+P = 128
+K = 1024
+NT = 64
+GT = 4
+NG = NT // GT
+XT_BUFS = 6
+X_BUFS = 12
+TQ = 16
+HALF = 32
+
+PIN = False
+B_ON_G = False
+V_COPIES = ()
+
+
+def tile_decoder_cross_projector_t_kernel(tc, node, node_mass, W, b, out):
+    nc = tc.nc
+    with ExitStack() as ctx:
+        const = ctx.enter_context(tc.tile_pool(name="const", bufs=1))
+        xpool = ctx.enter_context(tc.tile_pool(name="xpool", bufs=X_BUFS))
+        gpool = ctx.enter_context(tc.tile_pool(name="gpool", bufs=3))
+        rpool = ctx.enter_context(tc.tile_pool(name="rpool", bufs=3))
+        tpool = ctx.enter_context(tc.tile_pool(name="tpool", bufs=2))
+        xtp = ctx.enter_context(tc.psum_pool(name="xtp", bufs=XT_BUFS))
+        accp = ctx.enter_context(tc.psum_pool(name="accp", bufs=2))
+        if PIN:
+            ctx.enter_context(tc.manual_schedule())
+
+        node_v = node.rearrange("b (q i) k -> (b q) (i k)", i=NT)
+        mass_v = node_mass.rearrange("b (q i) -> (b q) i", i=NT)
+        out_v = out.rearrange("g b o (q i) d -> (b o q) g (i d)", i=NT)
+
+        mass_bf = const.tile([P, NT], BF16, name="mass_bf")
+        nc.scalar.dma_start(out=mass_bf[:], in_=mass_v)
+        wraw = const.tile([P, 1024], BF16, name="wraw")
+        nc.scalar.dma_start(
+            out=wraw[:].rearrange("p (c x) -> p c x", c=4),
+            in_=W.rearrange("(c p e) n -> p c (e n)", c=4, p=P, e=2),
+        )
+        brow = const.tile([P, P], BF16, name="brow")
+        nc.vector.memset(brow[:], 0.0)
+        nc.scalar.dma_start(out=brow[0:1, :], in_=b.rearrange("(o n) -> o n", o=1))
+
+        xs = {}
+
+        def load(c):
+            x = xpool.tile([P, GT * K], BF16, name="x", tag="x")
+            xs[c] = x
+            if c == 0:
+                for il in range(GT):
+                    nc.sync.dma_start(
+                        out=x[:, il * K : (il + 1) * K],
+                        in_=node_v[:, il * K : (il + 1) * K],
+                    )
+            else:
+                nc.sync.dma_start(out=x[:], in_=node_v[:, c * GT * K : (c + 1) * GT * K])
+
+        for c in range(X_BUFS):
+            load(c)
+
+        zero1 = const.tile([P, 1], F32, name="zero1")
+        nc.vector.memset(zero1[:], 0.0)
+        warm = const.tile([P, 1], F32, name="warm")
+        nc.scalar.activation(out=warm[:], in_=zero1[:], func=ACT.Sin)
+
+        ident = const.tile([P, P], F32, name="ident")
+        make_identity(nc, ident[:])
+
+        ones = const.tile([P, P], BF16, name="ones")
+        nc.vector.memset(ones[:], 1.0)
+
+        freq = const.tile([P, HALF], F32, name="freq")
+        nc.vector.memset(freq[:, 0:1], 1.0)
+        nc.vector.tensor_scalar(
+            out=freq[:, 0:1], in0=freq[:, 0:1], scalar1=1.0 / (2.0 * math.pi), scalar2=None, op0=ALU.mult
+        )
+        ratio = 10000.0 ** (-1.0 / HALF)
+        w = 1
+        while w < HALF:
+            nc.vector.tensor_scalar(
+                out=freq[:, w : 2 * w], in0=freq[:, 0:w], scalar1=ratio**w, scalar2=None, op0=ALU.mult
+            )
+            w *= 2
+        massf = const.tile([P, NT], F32, name="massf")
+        nc.vector.tensor_copy(out=massf[:], in_=mass_bf[:])
+
+        cs = const.tile([P, NT, 2, HALF], F32, name="cs")
+        trig = {}
+
+        def trig_g(q):
+            i0 = q * TQ
+            u = tpool.tile([P, TQ, HALF], F32, name="u", tag="u")
+            nn = tpool.tile([P, TQ, 2, HALF], I32, name="nn", tag="nn")
+            nc.gpsimd.tensor_tensor(
+                out=u[:],
+                in0=massf[:, i0 : i0 + TQ].unsqueeze(2).to_broadcast([P, TQ, HALF]),
+                in1=freq[:].unsqueeze(1).to_broadcast([P, TQ, HALF]),
+                op=ALU.mult,
+            )
+            nc.gpsimd.tensor_scalar(
+                out=nn[:, :, 0, :], in0=u[:], scalar1=1.0, scalar2=0.25, op0=ALU.mult, op1=ALU.add
+            )
+            nc.gpsimd.tensor_scalar(
+                out=nn[:, :, 1, :], in0=u[:], scalar1=1.0, scalar2=0.0, op0=ALU.mult, op1=ALU.add
+            )
+            trig[q] = (u, nn)
+
+        def trig_v(q):
+            u, nn = trig[q]
+            dd = tpool.tile([P, TQ, 2, HALF], F32, name="dd", tag="dd")
+            nc.vector.scalar_tensor_tensor(
+                out=dd[:, :, 0, :], in0=u[:], scalar=0.25, in1=nn[:, :, 0, :], op0=ALU.add, op1=ALU.subtract
+            )
+            nc.vector.tensor_tensor(out=dd[:, :, 1, :], in0=u[:], in1=nn[:, :, 1, :], op=ALU.subtract)
+            trig[q] = dd
+
+        def trig_s(q):
+            i0 = q * TQ
+            nc.scalar.activation(
+                out=cs[:, i0 : i0 + TQ, :, :], in_=trig[q][:], func=ACT.Sin, scale=2.0 * math.pi
+            )
+
+        trig_g(0)
+        trig_g(1)
+
+        wgrp = const.tile([P, 1024], BF16, name="wgrp", align_bytes=64)
+        nc.vector.tensor_copy(
+            out=wgrp[:].rearrange("p (g n t) -> p g n t", g=2, t=4),
+            in_=wraw[:].rearrange("p (g t n) -> p g n t", g=2, t=4),
+        )
+        wcodes = const.tile([P, 256], U32, name="wcodes", align_bytes=64)
+        wsc = const.tile([P, 256], U8, name="wsc", align_bytes=64)
+        trig_v(0)
+        nc.vector.quantize_mx(out=wcodes[:].bitcast(FP8X4), scales=wsc[:], in_=wgrp[:])
+
+        bps = accp.tile([P, 512], F32, name="bps", tag="acc")
+        nc.tensor.matmul(out=bps[:, 0:P], lhsT=ones[:], rhs=brow[:], start=True, stop=True)
+        bias = const.tile([P, P], F32, name="bias")
+        nc.vector.tensor_copy(out=bias[:], in_=bps[:, 0:P])
+
+        xts = {}
+        state = {"tb": 0}
+        grp = {}
+        accs = {}
+        res = {}
+
+        def transposes_upto(n):
+            while state["tb"] < min(n, NT):
+                bk = state["tb"]
+                xf = xs[bk // GT][:].bitcast(F32)
+                il = bk % GT
+                xt = xtp.tile([P, 512], F32, name="xt", tag="xt")
+                for wb in range(4):
+                    nc.tensor.transpose(
+                        xt[:, wb * P : (wb + 1) * P],
+                        xf[:, il * 512 + wb * P : il * 512 + (wb + 1) * P],
+                        ident[:],
+                    )
+                xts[bk] = xt
+                state["tb"] = bk + 1
+
+        def copy_out(bk):
+            c, il = bk // GT, bk % GT
+            if il == 0:
+                grp[c] = gpool.tile([P, GT * K], BF16, name="grouped", tag="grouped", align_bytes=64)
+            dst = grp[c][:].bitcast(F32)[:, il * 512 : (il + 1) * 512].rearrange(
+                "p (g t u) -> p g t u", g=2, u=2
+            )
+            src = xts[bk][:].rearrange("p (g u t) -> p g t u", g=2, u=2)
+            if bk in V_COPIES:
+                nc.vector.tensor_copy(out=dst, in_=src)
+            else:
+                nc.scalar.copy(out=dst, in_=src)
+
+        def quantise_and_multiply(c):
+            codes = gpool.tile([P, GT * 256], U32, name="codes", tag="codes", align_bytes=64)
+            sc = gpool.tile([P, GT * 256], U8, name="sc", tag="sc", align_bytes=64)
+            nc.vector.quantize_mx(out=codes[:].bitcast(FP8X4), scales=sc[:], in_=grp[c][:])
+            acc = accp.tile([P, 512], F32, name="acc", tag="acc")
+            for il in range(GT):
+                for g in range(2):
+                    o = (il * 2 + g) * P
+                    nc.tensor.matmul_mx(
+                        out=acc[:, il * P : (il + 1) * P],
+                        lhsT=codes[:, o : o + P].bitcast(FP8X4),
+                        lhsT_scale=sc[:, o : o + P],
+                        rhs=wcodes[:, g * P : (g + 1) * P].bitcast(FP8X4),
+                        rhs_scale=wsc[:, g * P : (g + 1) * P],
+                        start=(g == 0),
+                        stop=(g == 1),
+                    )
+            accs[c] = acc
+
+        def store_unit(c):
+            if c >= NG - 2:
+                return c, 1
+            return c - c % 2, 2
+
+        def epilogue(c):
+            c0, ng = store_unit(c)
+            if c == c0:
+                res[c0] = rpool.tile([P, 2, 2 * GT * 64], F32, name="res", tag="res")
+            r = res[c0]
+            off = (c - c0) * GT * 64
+            nc.vector.tensor_tensor(
+                out=r[:, :, off : off + GT * 64].rearrange("p g (i d) -> p i g d", d=64),
+                in0=accs[c][:].rearrange("p (i g d) -> p i g d", i=GT, g=2),
+                in1=bias[:].rearrange("p (g d) -> p g d", g=2).unsqueeze(1).to_broadcast([P, GT, 2, 64]),
+                op=ALU.add,
+            )
+            if c == c0 + ng - 1:
+                nt = ng * GT
+                i0 = c0 * GT
+                xh = r[:, 0, 0 : nt * 64].rearrange("p (i h j) -> p i h j", h=2, j=HALF)
+                ta = tpool.tile([P, 2 * GT, 2, HALF], F32, name="ta", tag="ta")
+                tb = tpool.tile([P, 2 * GT, 2, HALF], F32, name="tb", tag="tb")
+                cosv = cs[:, i0 : i0 + nt, 0:1, :].to_broadcast([P, nt, 2, HALF])
+                sinv = cs[:, i0 : i0 + nt, 1, :]
+                beng = nc.gpsimd if B_ON_G else nc.vector
+                beng.tensor_tensor(out=tb[:, 0:nt, 0, :], in0=xh[:, :, 1, :], in1=sinv, op=ALU.mult)
+                beng.tensor_tensor(out=tb[:, 0:nt, 1, :], in0=xh[:, :, 0, :], in1=sinv, op=ALU.mult)
+                nc.vector.tensor_tensor(out=ta[:, 0:nt, :, :], in0=xh, in1=cosv, op=ALU.mult)
+                nc.vector.tensor_tensor(
+                    out=xh[:, :, 0, :], in0=ta[:, 0:nt, 0, :], in1=tb[:, 0:nt, 0, :], op=ALU.subtract
+                )
+                nc.vector.tensor_tensor(
+                    out=xh[:, :, 1, :], in0=ta[:, 0:nt, 1, :], in1=tb[:, 0:nt, 1, :], op=ALU.add
+                )
+                n = ng * GT * 64
+                nc.sync.dma_start(
+                    out=out_v[:, :, c0 * GT * 64 : c0 * GT * 64 + n], in_=r[:, :, 0:n]
+                )
+
+        transposes_upto(XT_BUFS)
+        for c in range(NG):
+            for il in range(GT):
+                bk = c * GT + il
+                copy_out(bk)
+                transposes_upto(bk + XT_BUFS + 1)
+            if c % 4 == 0:
+                trig_s(c // 4)
+            quantise_and_multiply(c)
+            if c >= 1:
+                epilogue(c - 1)
+            if c % 4 == 1 and c // 4 + 2 < NT // TQ:
+                trig_g(c // 4 + 2)
+            if c % 4 == 1 and c // 4 + 1 < NT // TQ:
+                trig_v(c // 4 + 1)
+            if c + X_BUFS < NG:
+                load(c + X_BUFS)
+        epilogue(NG - 1)

@@ -25,7 +25,9 @@ X_BUFS = 12
 TQ = 16
 HALF = 32
 
-PIN = False
+PIN = True
+NW = 4
+ND = 4
 B_ON_G = False
 V_COPIES = ()
 
@@ -85,6 +87,8 @@ def tile_decoder_cross_projector_t_kernel(tc, node, node_mass, W, b, out):
 
         ones = const.tile([P, P], BF16, name="ones")
         nc.vector.memset(ones[:], 1.0)
+        wz = const.tile([P, 512], BF16, name="wz")
+        nc.vector.memset(wz[:], 0.0)
 
         freq = const.tile([P, HALF], F32, name="freq")
         nc.vector.memset(freq[:, 0:1], 1.0)
@@ -106,8 +110,8 @@ def tile_decoder_cross_projector_t_kernel(tc, node, node_mass, W, b, out):
 
         def trig_g(q):
             i0 = q * TQ
-            u = tpool.tile([P, TQ, HALF], F32, name="u", tag="u")
-            nn = tpool.tile([P, TQ, 2, HALF], I32, name="nn", tag="nn")
+            u = tpool.tile([P, TQ, HALF], F32, name="u", tag="u", bufs=4)
+            nn = tpool.tile([P, TQ, 2, HALF], I32, name="nn", tag="nn", bufs=4)
             nc.gpsimd.tensor_tensor(
                 out=u[:],
                 in0=massf[:, i0 : i0 + TQ].unsqueeze(2).to_broadcast([P, TQ, HALF]),
@@ -137,8 +141,8 @@ def tile_decoder_cross_projector_t_kernel(tc, node, node_mass, W, b, out):
                 out=cs[:, i0 : i0 + TQ, :, :], in_=trig[q][:], func=ACT.Sin, scale=2.0 * math.pi
             )
 
-        trig_g(0)
-        trig_g(1)
+        for q in range(NT // TQ):
+            trig_g(q)
 
         wgrp = const.tile([P, 1024], BF16, name="wgrp", align_bytes=64)
         nc.vector.tensor_copy(
@@ -147,13 +151,15 @@ def tile_decoder_cross_projector_t_kernel(tc, node, node_mass, W, b, out):
         )
         wcodes = const.tile([P, 256], U32, name="wcodes", align_bytes=64)
         wsc = const.tile([P, 256], U8, name="wsc", align_bytes=64)
-        trig_v(0)
         nc.vector.quantize_mx(out=wcodes[:].bitcast(FP8X4), scales=wsc[:], in_=wgrp[:])
 
         bps = accp.tile([P, 512], F32, name="bps", tag="acc")
+        for r in range(NW):
+            nc.tensor.matmul(out=bps[:], lhsT=ones[:], rhs=wz[:], start=True, stop=True)
         nc.tensor.matmul(out=bps[:, 0:P], lhsT=ones[:], rhs=brow[:], start=True, stop=True)
         bias = const.tile([P, P], F32, name="bias")
         nc.vector.tensor_copy(out=bias[:], in_=bps[:, 0:P])
+        trig_v(0)
 
         xts = {}
         state = {"tb": 0}
@@ -194,6 +200,16 @@ def tile_decoder_cross_projector_t_kernel(tc, node, node_mass, W, b, out):
             sc = gpool.tile([P, GT * 256], U8, name="sc", tag="sc", align_bytes=64)
             nc.vector.quantize_mx(out=codes[:].bitcast(FP8X4), scales=sc[:], in_=grp[c][:])
             acc = accp.tile([P, 512], F32, name="acc", tag="acc")
+            for r in range(ND):
+                nc.tensor.matmul_mx(
+                    out=acc[:, 0:256],
+                    lhsT=wcodes[:, 0:P].bitcast(FP8X4),
+                    lhsT_scale=wsc[:, 0:P],
+                    rhs=wcodes[:].bitcast(FP8X4),
+                    rhs_scale=wsc[:],
+                    start=True,
+                    stop=True,
+                )
             for il in range(GT):
                 for g in range(2):
                     o = (il * 2 + g) * P
@@ -259,8 +275,6 @@ def tile_decoder_cross_projector_t_kernel(tc, node, node_mass, W, b, out):
             quantise_and_multiply(c)
             if c >= 1:
                 epilogue(c - 1)
-            if c % 4 == 1 and c // 4 + 2 < NT // TQ:
-                trig_g(c // 4 + 2)
             if c % 4 == 1 and c // 4 + 1 < NT // TQ:
                 trig_v(c // 4 + 1)
             if c + X_BUFS < NG:

@@ -28,8 +28,9 @@ HALF = 32
 PIN = True
 NW = 4
 ND = 4
-B_ON_G = False
 V_COPIES = ()
+TRIG_ITER = {2: 0, 4: 1, 8: 2, 12: 3}
+UNITS = ((0, 2), (2, 2), (4, 2), (6, 2), (8, 2), (10, 2), (12, 2), (14, 1), (15, 1))
 
 
 def tile_decoder_cross_projector_t_kernel(tc, node, node_mass, W, b, out):
@@ -38,7 +39,7 @@ def tile_decoder_cross_projector_t_kernel(tc, node, node_mass, W, b, out):
         const = ctx.enter_context(tc.tile_pool(name="const", bufs=1))
         xpool = ctx.enter_context(tc.tile_pool(name="xpool", bufs=X_BUFS))
         gpool = ctx.enter_context(tc.tile_pool(name="gpool", bufs=3))
-        rpool = ctx.enter_context(tc.tile_pool(name="rpool", bufs=3))
+        rpool = ctx.enter_context(tc.tile_pool(name="rpool", bufs=4))
         tpool = ctx.enter_context(tc.tile_pool(name="tpool", bufs=2))
         xtp = ctx.enter_context(tc.psum_pool(name="xtp", bufs=XT_BUFS))
         accp = ctx.enter_context(tc.psum_pool(name="accp", bufs=2))
@@ -89,6 +90,8 @@ def tile_decoder_cross_projector_t_kernel(tc, node, node_mass, W, b, out):
         nc.vector.memset(ones[:], 1.0)
         wz = const.tile([P, 512], BF16, name="wz")
         nc.vector.memset(wz[:], 0.0)
+        q25 = const.tile([P, 1], F32, name="q25")
+        nc.vector.memset(q25[:], 0.25)
 
         freq = const.tile([P, HALF], F32, name="freq")
         nc.vector.memset(freq[:, 0:1], 1.0)
@@ -105,53 +108,24 @@ def tile_decoder_cross_projector_t_kernel(tc, node, node_mass, W, b, out):
         massf = const.tile([P, NT], F32, name="massf")
         nc.vector.tensor_copy(out=massf[:], in_=mass_bf[:])
 
-        cs = const.tile([P, NT, 2, HALF], F32, name="cs")
-        trig = {}
-
-        def trig_g(q):
-            i0 = q * TQ
-            u = tpool.tile([P, TQ, HALF], F32, name="u", tag="u", bufs=4)
-            nn = tpool.tile([P, TQ, 2, HALF], I32, name="nn", tag="nn", bufs=4)
-            nc.gpsimd.tensor_tensor(
-                out=u[:],
-                in0=massf[:, i0 : i0 + TQ].unsqueeze(2).to_broadcast([P, TQ, HALF]),
-                in1=freq[:].unsqueeze(1).to_broadcast([P, TQ, HALF]),
-                op=ALU.mult,
-            )
-            nc.gpsimd.tensor_scalar(
-                out=nn[:, :, 0, :], in0=u[:], scalar1=1.0, scalar2=0.25, op0=ALU.mult, op1=ALU.add
-            )
-            nc.gpsimd.tensor_scalar(
-                out=nn[:, :, 1, :], in0=u[:], scalar1=1.0, scalar2=0.0, op0=ALU.mult, op1=ALU.add
-            )
-            trig[q] = (u, nn)
-
-        def trig_v(q):
-            u, nn = trig[q]
-            dd = tpool.tile([P, TQ, 2, HALF], F32, name="dd", tag="dd")
-            nc.vector.scalar_tensor_tensor(
-                out=dd[:, :, 0, :], in0=u[:], scalar=0.25, in1=nn[:, :, 0, :], op0=ALU.add, op1=ALU.subtract
-            )
-            nc.vector.tensor_tensor(out=dd[:, :, 1, :], in0=u[:], in1=nn[:, :, 1, :], op=ALU.subtract)
-            trig[q] = dd
-
-        def trig_s(q):
-            i0 = q * TQ
-            nc.scalar.activation(
-                out=cs[:, i0 : i0 + TQ, :, :], in_=trig[q][:], func=ACT.Sin, scale=2.0 * math.pi
-            )
-
-        for q in range(NT // TQ):
-            trig_g(q)
-
+        turns = const.tile([P, NT, HALF], F32, name="turns")
+        whole = const.tile([P, NT, HALF], I32, name="whole")
+        nc.vector.tensor_tensor(
+            out=turns[:],
+            in0=massf[:].unsqueeze(2).to_broadcast([P, NT, HALF]),
+            in1=freq[:].unsqueeze(1).to_broadcast([P, NT, HALF]),
+            op=ALU.mult,
+        )
         wgrp = const.tile([P, 1024], BF16, name="wgrp", align_bytes=64)
         nc.vector.tensor_copy(
             out=wgrp[:].rearrange("p (g n t) -> p g n t", g=2, t=4),
             in_=wraw[:].rearrange("p (g t n) -> p g n t", g=2, t=4),
         )
+        nc.vector.tensor_copy(out=whole[:], in_=turns[:])
         wcodes = const.tile([P, 256], U32, name="wcodes", align_bytes=64)
         wsc = const.tile([P, 256], U8, name="wsc", align_bytes=64)
         nc.vector.quantize_mx(out=wcodes[:].bitcast(FP8X4), scales=wsc[:], in_=wgrp[:])
+        nc.vector.tensor_tensor(out=turns[:], in0=turns[:], in1=whole[:], op=ALU.subtract)
 
         bps = accp.tile([P, 512], F32, name="bps", tag="acc")
         for r in range(NW):
@@ -159,13 +133,34 @@ def tile_decoder_cross_projector_t_kernel(tc, node, node_mass, W, b, out):
         nc.tensor.matmul(out=bps[:, 0:P], lhsT=ones[:], rhs=brow[:], start=True, stop=True)
         bias = const.tile([P, P], F32, name="bias")
         nc.vector.tensor_copy(out=bias[:], in_=bps[:, 0:P])
-        trig_v(0)
+
+        cs = const.tile([P, NT, 2, HALF], F32, name="cs")
+        tmp = {}
+
+        def trig_s(q, step):
+            i0 = q * TQ
+            d = turns[:, i0 : i0 + TQ, :]
+            if step == 0:
+                nc.scalar.activation(out=cs[:, i0 : i0 + TQ, 1, :], in_=d, func=ACT.Sin, scale=2.0 * math.pi)
+            elif step == 1:
+                tmp["a"] = tpool.tile([P, TQ, HALF], F32, name="ab", tag="ab")
+                nc.scalar.activation(out=tmp["a"][:], in_=d, func=ACT.Abs)
+            elif step == 2:
+                tmp["z"] = tpool.tile([P, TQ, HALF], F32, name="zz", tag="zz")
+                nc.scalar.activation(
+                    out=tmp["z"][:], in_=tmp["a"][:], func=ACT.Identity, scale=-1.0, bias=q25[:]
+                )
+            else:
+                nc.scalar.activation(
+                    out=cs[:, i0 : i0 + TQ, 0, :], in_=tmp["z"][:], func=ACT.Sin, scale=2.0 * math.pi
+                )
 
         xts = {}
         state = {"tb": 0}
         grp = {}
         accs = {}
         res = {}
+        prod = {}
 
         def transposes_upto(n):
             while state["tb"] < min(n, NT):
@@ -224,45 +219,60 @@ def tile_decoder_cross_projector_t_kernel(tc, node, node_mass, W, b, out):
                     )
             accs[c] = acc
 
-        def store_unit(c):
-            if c >= NG - 2:
-                return c, 1
-            return c - c % 2, 2
+        unit_of = {}
+        for k, (c0, ng) in enumerate(UNITS):
+            for c in range(c0, c0 + ng):
+                unit_of[c] = k
 
-        def epilogue(c):
-            c0, ng = store_unit(c)
+        def add_bias(c):
+            k = unit_of[c]
+            c0, ng = UNITS[k]
             if c == c0:
-                res[c0] = rpool.tile([P, 2, 2 * GT * 64], F32, name="res", tag="res")
-            r = res[c0]
+                res[k] = rpool.tile([P, 2, 2 * GT * 64], F32, name="res", tag="res")
             off = (c - c0) * GT * 64
             nc.vector.tensor_tensor(
-                out=r[:, :, off : off + GT * 64].rearrange("p g (i d) -> p i g d", d=64),
+                out=res[k][:, :, off : off + GT * 64].rearrange("p g (i d) -> p i g d", d=64),
                 in0=accs[c][:].rearrange("p (i g d) -> p i g d", i=GT, g=2),
                 in1=bias[:].rearrange("p (g d) -> p g d", g=2).unsqueeze(1).to_broadcast([P, GT, 2, 64]),
                 op=ALU.add,
             )
-            if c == c0 + ng - 1:
-                nt = ng * GT
-                i0 = c0 * GT
-                xh = r[:, 0, 0 : nt * 64].rearrange("p (i h j) -> p i h j", h=2, j=HALF)
-                ta = tpool.tile([P, 2 * GT, 2, HALF], F32, name="ta", tag="ta")
-                tb = tpool.tile([P, 2 * GT, 2, HALF], F32, name="tb", tag="tb")
-                cosv = cs[:, i0 : i0 + nt, 0:1, :].to_broadcast([P, nt, 2, HALF])
-                sinv = cs[:, i0 : i0 + nt, 1, :]
-                beng = nc.gpsimd if B_ON_G else nc.vector
-                beng.tensor_tensor(out=tb[:, 0:nt, 0, :], in0=xh[:, :, 1, :], in1=sinv, op=ALU.mult)
-                beng.tensor_tensor(out=tb[:, 0:nt, 1, :], in0=xh[:, :, 0, :], in1=sinv, op=ALU.mult)
-                nc.vector.tensor_tensor(out=ta[:, 0:nt, :, :], in0=xh, in1=cosv, op=ALU.mult)
-                nc.vector.tensor_tensor(
-                    out=xh[:, :, 0, :], in0=ta[:, 0:nt, 0, :], in1=tb[:, 0:nt, 0, :], op=ALU.subtract
-                )
-                nc.vector.tensor_tensor(
-                    out=xh[:, :, 1, :], in0=ta[:, 0:nt, 1, :], in1=tb[:, 0:nt, 1, :], op=ALU.add
-                )
-                n = ng * GT * 64
-                nc.sync.dma_start(
-                    out=out_v[:, :, c0 * GT * 64 : c0 * GT * 64 + n], in_=r[:, :, 0:n]
-                )
+
+        def products(k):
+            c0, ng = UNITS[k]
+            nt = ng * GT
+            i0 = c0 * GT
+            xh = res[k][:, 0, 0 : nt * 64].rearrange("p (i h j) -> p i h j", h=2, j=HALF)
+            ta = tpool.tile([P, 2 * GT, 2, HALF], F32, name="ta", tag="ta")
+            tb = tpool.tile([P, 2 * GT, 2, HALF], F32, name="tb", tag="tb")
+            cosv = cs[:, i0 : i0 + nt, 0:1, :].to_broadcast([P, nt, 2, HALF])
+            sinv = cs[:, i0 : i0 + nt, 1, :]
+            nc.vector.tensor_tensor(out=tb[:, 0:nt, 0, :], in0=xh[:, :, 1, :], in1=sinv, op=ALU.mult)
+            nc.vector.tensor_tensor(out=tb[:, 0:nt, 1, :], in0=xh[:, :, 0, :], in1=sinv, op=ALU.mult)
+            nc.vector.tensor_tensor(out=ta[:, 0:nt, :, :], in0=xh, in1=cosv, op=ALU.mult)
+            prod[k] = (ta, tb)
+
+        def sums_and_store(k):
+            c0, ng = UNITS[k]
+            nt = ng * GT
+            xh = res[k][:, 0, 0 : nt * 64].rearrange("p (i h j) -> p i h j", h=2, j=HALF)
+            ta, tb = prod[k]
+            nc.vector.tensor_tensor(
+                out=xh[:, :, 0, :], in0=ta[:, 0:nt, 0, :], in1=tb[:, 0:nt, 0, :], op=ALU.subtract
+            )
+            nc.vector.tensor_tensor(out=xh[:, :, 1, :], in0=ta[:, 0:nt, 1, :], in1=tb[:, 0:nt, 1, :], op=ALU.add)
+            n = nt * 64
+            nc.sync.dma_start(out=out_v[:, :, c0 * GT * 64 : c0 * GT * 64 + n], in_=res[k][:, :, 0:n])
+
+        todo = []
+        done = {"n": 0}
+
+        def next_half():
+            kind, k = todo[done["n"]]
+            done["n"] += 1
+            if kind == "p":
+                products(k)
+            else:
+                sums_and_store(k)
 
         transposes_upto(XT_BUFS)
         for c in range(NG):
@@ -270,13 +280,22 @@ def tile_decoder_cross_projector_t_kernel(tc, node, node_mass, W, b, out):
                 bk = c * GT + il
                 copy_out(bk)
                 transposes_upto(bk + XT_BUFS + 1)
-            if c % 4 == 0:
-                trig_s(c // 4)
+                if c in TRIG_ITER:
+                    trig_s(TRIG_ITER[c], il)
             quantise_and_multiply(c)
+            ready = len(todo) > done["n"]
             if c >= 1:
-                epilogue(c - 1)
-            if c % 4 == 1 and c // 4 + 1 < NT // TQ:
-                trig_v(c // 4 + 1)
+                add_bias(c - 1)
+                k = unit_of[c - 1]
+                if c - 1 == UNITS[k][0] + UNITS[k][1] - 1:
+                    todo.append(("p", k))
+                    todo.append(("s", k))
+            if ready:
+                next_half()
             if c + X_BUFS < NG:
                 load(c + X_BUFS)
-        epilogue(NG - 1)
+        add_bias(NG - 1)
+        todo.append(("p", unit_of[NG - 1]))
+        todo.append(("s", unit_of[NG - 1]))
+        while done["n"] < len(todo):
+            next_half()

@@ -26,8 +26,8 @@ TQ = 16
 HALF = 32
 
 PIN = True
-NW = 4
-ND = 4
+NW = 0
+ND = 0
 V_COPIES = ()
 TRIG_ITER = {2: 0, 4: 1, 8: 2, 12: 3}
 UNITS = ((0, 2), (2, 2), (4, 2), (6, 2), (8, 2), (10, 2), (12, 2), (14, 1), (15, 1))

@@ -18,19 +18,21 @@ ACT = mybir.ActivationFunctionType
 P = 128
 K = 1024
 NT = 64
-GT = 4
-NG = NT // GT
+LT = 4
+NL = NT // LT
 XT_BUFS = 6
-X_BUFS = 12
+X_BUFS = 10
 TQ = 16
 HALF = 32
 
-PIN = True
-NW = 0
-ND = 0
-V_COPIES = ()
-TRIG_ITER = {2: 0, 4: 1, 8: 2, 12: 3}
-UNITS = ((0, 2), (2, 2), (4, 2), (6, 2), (8, 2), (10, 2), (12, 2), (14, 1), (15, 1))
+GROUPS = (
+    (0, 1), (1, 1), (2, 2), (4, 4), (8, 4), (12, 4), (16, 4), (20, 4), (24, 4), (28, 4), (32, 4),
+    (36, 4), (40, 4), (44, 4), (48, 4), (52, 4), (56, 4), (60, 2), (62, 1), (63, 1),
+)
+UNITS = ((0, 8), (8, 8), (16, 8), (24, 8), (32, 8), (40, 8), (48, 8), (56, 4), (60, 2), (62, 2))
+SUB_AT = {1: 0, 2: 1, 3: 2, 4: 3}
+TRIG_AT = {3: 0, 5: 1, 8: 2, 12: 3}
+SPLIT_LOADS = (0, NL - 1)
 
 
 def tile_decoder_cross_projector_t_kernel(tc, node, node_mass, W, b, out):
@@ -43,8 +45,7 @@ def tile_decoder_cross_projector_t_kernel(tc, node, node_mass, W, b, out):
         tpool = ctx.enter_context(tc.tile_pool(name="tpool", bufs=2))
         xtp = ctx.enter_context(tc.psum_pool(name="xtp", bufs=XT_BUFS))
         accp = ctx.enter_context(tc.psum_pool(name="accp", bufs=2))
-        if PIN:
-            ctx.enter_context(tc.manual_schedule())
+        ctx.enter_context(tc.manual_schedule())
 
         node_v = node.rearrange("b (q i) k -> (b q) (i k)", i=NT)
         mass_v = node_mass.rearrange("b (q i) -> (b q) i", i=NT)
@@ -63,20 +64,20 @@ def tile_decoder_cross_projector_t_kernel(tc, node, node_mass, W, b, out):
 
         xs = {}
 
-        def load(c):
-            x = xpool.tile([P, GT * K], BF16, name="x", tag="x")
-            xs[c] = x
-            if c == 0:
-                for il in range(GT):
+        def load(l):
+            x = xpool.tile([P, LT * K], BF16, name="x", tag="x")
+            xs[l] = x
+            if l in SPLIT_LOADS:
+                for il in range(LT):
                     nc.sync.dma_start(
                         out=x[:, il * K : (il + 1) * K],
-                        in_=node_v[:, il * K : (il + 1) * K],
+                        in_=node_v[:, (l * LT + il) * K : (l * LT + il + 1) * K],
                     )
             else:
-                nc.sync.dma_start(out=x[:], in_=node_v[:, c * GT * K : (c + 1) * GT * K])
+                nc.sync.dma_start(out=x[:], in_=node_v[:, l * LT * K : (l + 1) * LT * K])
 
-        for c in range(X_BUFS):
-            load(c)
+        for l in range(X_BUFS):
+            load(l)
 
         zero1 = const.tile([P, 1], F32, name="zero1")
         nc.vector.memset(zero1[:], 0.0)
@@ -88,8 +89,6 @@ def tile_decoder_cross_projector_t_kernel(tc, node, node_mass, W, b, out):
 
         ones = const.tile([P, P], BF16, name="ones")
         nc.vector.memset(ones[:], 1.0)
-        wz = const.tile([P, 512], BF16, name="wz")
-        nc.vector.memset(wz[:], 0.0)
         q25 = const.tile([P, 1], F32, name="q25")
         nc.vector.memset(q25[:], 0.25)
 
@@ -105,34 +104,50 @@ def tile_decoder_cross_projector_t_kernel(tc, node, node_mass, W, b, out):
                 out=freq[:, w : 2 * w], in0=freq[:, 0:w], scalar1=ratio**w, scalar2=None, op0=ALU.mult
             )
             w *= 2
-        massf = const.tile([P, NT], F32, name="massf")
-        nc.vector.tensor_copy(out=massf[:], in_=mass_bf[:])
 
+        massf = const.tile([P, NT], F32, name="massf")
+        nc.gpsimd.tensor_copy(out=massf[:], in_=mass_bf[:])
         turns = const.tile([P, NT, HALF], F32, name="turns")
         whole = const.tile([P, NT, HALF], I32, name="whole")
-        nc.vector.tensor_tensor(
-            out=turns[:],
-            in0=massf[:].unsqueeze(2).to_broadcast([P, NT, HALF]),
-            in1=freq[:].unsqueeze(1).to_broadcast([P, NT, HALF]),
-            op=ALU.mult,
-        )
+        for q in range(NT // TQ):
+            i0 = q * TQ
+            nc.gpsimd.tensor_tensor(
+                out=turns[:, i0 : i0 + TQ, :],
+                in0=massf[:, i0 : i0 + TQ].unsqueeze(2).to_broadcast([P, TQ, HALF]),
+                in1=freq[:].unsqueeze(1).to_broadcast([P, TQ, HALF]),
+                op=ALU.mult,
+            )
+            nc.gpsimd.tensor_scalar(
+                out=whole[:, i0 : i0 + TQ, :],
+                in0=turns[:, i0 : i0 + TQ, :],
+                scalar1=1.0,
+                scalar2=0.0,
+                op0=ALU.mult,
+                op1=ALU.add,
+            )
+
+        def reduce_angles(q):
+            i0 = q * TQ
+            nc.vector.tensor_tensor(
+                out=turns[:, i0 : i0 + TQ, :],
+                in0=turns[:, i0 : i0 + TQ, :],
+                in1=whole[:, i0 : i0 + TQ, :],
+                op=ALU.subtract,
+            )
+
         wgrp = const.tile([P, 1024], BF16, name="wgrp", align_bytes=64)
         nc.vector.tensor_copy(
             out=wgrp[:].rearrange("p (g n t) -> p g n t", g=2, t=4),
             in_=wraw[:].rearrange("p (g t n) -> p g n t", g=2, t=4),
         )
-        nc.vector.tensor_copy(out=whole[:], in_=turns[:])
         wcodes = const.tile([P, 256], U32, name="wcodes", align_bytes=64)
         wsc = const.tile([P, 256], U8, name="wsc", align_bytes=64)
         nc.vector.quantize_mx(out=wcodes[:].bitcast(FP8X4), scales=wsc[:], in_=wgrp[:])
-        nc.vector.tensor_tensor(out=turns[:], in0=turns[:], in1=whole[:], op=ALU.subtract)
 
         bps = accp.tile([P, 512], F32, name="bps", tag="acc")
-        for r in range(NW):
-            nc.tensor.matmul(out=bps[:], lhsT=ones[:], rhs=wz[:], start=True, stop=True)
         nc.tensor.matmul(out=bps[:, 0:P], lhsT=ones[:], rhs=brow[:], start=True, stop=True)
         bias = const.tile([P, P], F32, name="bias")
-        nc.vector.tensor_copy(out=bias[:], in_=bps[:, 0:P])
+        nc.scalar.copy(out=bias[:], in_=bps[:, 0:P])
 
         cs = const.tile([P, NT, 2, HALF], F32, name="cs")
         tmp = {}
@@ -156,17 +171,26 @@ def tile_decoder_cross_projector_t_kernel(tc, node, node_mass, W, b, out):
                 )
 
         xts = {}
-        state = {"tb": 0}
+        state = {"tb": 0, "half": 0}
         grp = {}
+        qnt = {}
         accs = {}
         res = {}
         prod = {}
+        group_of = {}
+        for s, (t0, nt) in enumerate(GROUPS):
+            for t in range(t0, t0 + nt):
+                group_of[t] = s
+        unit_of = {}
+        for k, (t0, nt) in enumerate(UNITS):
+            for t in range(t0, t0 + nt):
+                unit_of[group_of[t]] = k
 
         def transposes_upto(n):
             while state["tb"] < min(n, NT):
                 bk = state["tb"]
-                xf = xs[bk // GT][:].bitcast(F32)
-                il = bk % GT
+                xf = xs[bk // LT][:].bitcast(F32)
+                il = bk % LT
                 xt = xtp.tile([P, 512], F32, name="xt", tag="xt")
                 for wb in range(4):
                     nc.tensor.transpose(
@@ -176,36 +200,33 @@ def tile_decoder_cross_projector_t_kernel(tc, node, node_mass, W, b, out):
                     )
                 xts[bk] = xt
                 state["tb"] = bk + 1
+                if il == LT - 1 and bk // LT + X_BUFS < NL:
+                    load(bk // LT + X_BUFS)
 
         def copy_out(bk):
-            c, il = bk // GT, bk % GT
+            s = group_of[bk]
+            il = bk - GROUPS[s][0]
             if il == 0:
-                grp[c] = gpool.tile([P, GT * K], BF16, name="grouped", tag="grouped", align_bytes=64)
-            dst = grp[c][:].bitcast(F32)[:, il * 512 : (il + 1) * 512].rearrange(
+                grp[s] = gpool.tile([P, 4 * K], BF16, name="grouped", tag="grouped", bufs=5, align_bytes=64)
+            dst = grp[s][:].bitcast(F32)[:, il * 512 : (il + 1) * 512].rearrange(
                 "p (g t u) -> p g t u", g=2, u=2
             )
-            src = xts[bk][:].rearrange("p (g u t) -> p g t u", g=2, u=2)
-            if bk in V_COPIES:
-                nc.vector.tensor_copy(out=dst, in_=src)
-            else:
-                nc.scalar.copy(out=dst, in_=src)
+            nc.scalar.copy(out=dst, in_=xts[bk][:].rearrange("p (g u t) -> p g t u", g=2, u=2))
 
-        def quantise_and_multiply(c):
-            codes = gpool.tile([P, GT * 256], U32, name="codes", tag="codes", align_bytes=64)
-            sc = gpool.tile([P, GT * 256], U8, name="sc", tag="sc", align_bytes=64)
-            nc.vector.quantize_mx(out=codes[:].bitcast(FP8X4), scales=sc[:], in_=grp[c][:])
+        def quantise(s):
+            nt = GROUPS[s][1]
+            codes = gpool.tile([P, 4 * 256], U32, name="codes", tag="codes", align_bytes=64)
+            sc = gpool.tile([P, 4 * 256], U8, name="sc", tag="sc", align_bytes=64)
+            nc.vector.quantize_mx(
+                out=codes[:, 0 : nt * 256].bitcast(FP8X4), scales=sc[:, 0 : nt * 256], in_=grp[s][:, 0 : nt * K]
+            )
+            qnt[s] = (codes, sc)
+
+        def multiply(s):
+            nt = GROUPS[s][1]
+            codes, sc = qnt[s]
             acc = accp.tile([P, 512], F32, name="acc", tag="acc")
-            for r in range(ND):
-                nc.tensor.matmul_mx(
-                    out=acc[:, 0:256],
-                    lhsT=wcodes[:, 0:P].bitcast(FP8X4),
-                    lhsT_scale=wsc[:, 0:P],
-                    rhs=wcodes[:].bitcast(FP8X4),
-                    rhs_scale=wsc[:],
-                    start=True,
-                    stop=True,
-                )
-            for il in range(GT):
+            for il in range(nt):
                 for g in range(2):
                     o = (il * 2 + g) * P
                     nc.tensor.matmul_mx(
@@ -217,33 +238,32 @@ def tile_decoder_cross_projector_t_kernel(tc, node, node_mass, W, b, out):
                         start=(g == 0),
                         stop=(g == 1),
                     )
-            accs[c] = acc
+            accs[s] = acc
 
-        unit_of = {}
-        for k, (c0, ng) in enumerate(UNITS):
-            for c in range(c0, c0 + ng):
-                unit_of[c] = k
+        todo = []
 
-        def add_bias(c):
-            k = unit_of[c]
-            c0, ng = UNITS[k]
-            if c == c0:
-                res[k] = rpool.tile([P, 2, 2 * GT * 64], F32, name="res", tag="res")
-            off = (c - c0) * GT * 64
+        def add_bias(s):
+            t0, nt = GROUPS[s]
+            k = unit_of[s]
+            u0, un = UNITS[k]
+            if t0 == u0:
+                res[k] = rpool.tile([P, 2, 8 * 64], F32, name="res", tag="res")
+            off = (t0 - u0) * 64
             nc.vector.tensor_tensor(
-                out=res[k][:, :, off : off + GT * 64].rearrange("p g (i d) -> p i g d", d=64),
-                in0=accs[c][:].rearrange("p (i g d) -> p i g d", i=GT, g=2),
-                in1=bias[:].rearrange("p (g d) -> p g d", g=2).unsqueeze(1).to_broadcast([P, GT, 2, 64]),
+                out=res[k][:, :, off : off + nt * 64].rearrange("p g (i d) -> p i g d", d=64),
+                in0=accs[s][:, 0 : nt * P].rearrange("p (i g d) -> p i g d", i=nt, g=2),
+                in1=bias[:].rearrange("p (g d) -> p g d", g=2).unsqueeze(1).to_broadcast([P, nt, 2, 64]),
                 op=ALU.add,
             )
+            if t0 + nt == u0 + un:
+                todo.append(("p", k))
+                todo.append(("s", k))
 
         def products(k):
-            c0, ng = UNITS[k]
-            nt = ng * GT
-            i0 = c0 * GT
+            i0, nt = UNITS[k]
             xh = res[k][:, 0, 0 : nt * 64].rearrange("p (i h j) -> p i h j", h=2, j=HALF)
-            ta = tpool.tile([P, 2 * GT, 2, HALF], F32, name="ta", tag="ta")
-            tb = tpool.tile([P, 2 * GT, 2, HALF], F32, name="tb", tag="tb")
+            ta = tpool.tile([P, 8, 2, HALF], F32, name="ta", tag="ta")
+            tb = tpool.tile([P, 8, 2, HALF], F32, name="tb", tag="tb")
             cosv = cs[:, i0 : i0 + nt, 0:1, :].to_broadcast([P, nt, 2, HALF])
             sinv = cs[:, i0 : i0 + nt, 1, :]
             nc.vector.tensor_tensor(out=tb[:, 0:nt, 0, :], in0=xh[:, :, 1, :], in1=sinv, op=ALU.mult)
@@ -252,50 +272,53 @@ def tile_decoder_cross_projector_t_kernel(tc, node, node_mass, W, b, out):
             prod[k] = (ta, tb)
 
         def sums_and_store(k):
-            c0, ng = UNITS[k]
-            nt = ng * GT
+            i0, nt = UNITS[k]
             xh = res[k][:, 0, 0 : nt * 64].rearrange("p (i h j) -> p i h j", h=2, j=HALF)
             ta, tb = prod[k]
             nc.vector.tensor_tensor(
                 out=xh[:, :, 0, :], in0=ta[:, 0:nt, 0, :], in1=tb[:, 0:nt, 0, :], op=ALU.subtract
             )
             nc.vector.tensor_tensor(out=xh[:, :, 1, :], in0=ta[:, 0:nt, 1, :], in1=tb[:, 0:nt, 1, :], op=ALU.add)
-            n = nt * 64
-            nc.sync.dma_start(out=out_v[:, :, c0 * GT * 64 : c0 * GT * 64 + n], in_=res[k][:, :, 0:n])
-
-        todo = []
-        done = {"n": 0}
+            nc.sync.dma_start(out=out_v[:, :, i0 * 64 : (i0 + nt) * 64], in_=res[k][:, :, 0 : nt * 64])
 
         def next_half():
-            kind, k = todo[done["n"]]
-            done["n"] += 1
+            kind, k = todo[state["half"]]
+            state["half"] += 1
             if kind == "p":
                 products(k)
             else:
                 sums_and_store(k)
 
+        ns = len(GROUPS)
+        strig = []
+        sdone = {"n": 0}
         transposes_upto(XT_BUFS)
-        for c in range(NG):
-            for il in range(GT):
-                bk = c * GT + il
+        for s in range(ns):
+            t0, nt = GROUPS[s]
+            if s in TRIG_AT:
+                for step in range(4):
+                    strig.append((TRIG_AT[s], step))
+            for bk in range(t0, t0 + nt):
                 copy_out(bk)
                 transposes_upto(bk + XT_BUFS + 1)
-                if c in TRIG_ITER:
-                    trig_s(TRIG_ITER[c], il)
-            quantise_and_multiply(c)
-            ready = len(todo) > done["n"]
-            if c >= 1:
-                add_bias(c - 1)
-                k = unit_of[c - 1]
-                if c - 1 == UNITS[k][0] + UNITS[k][1] - 1:
-                    todo.append(("p", k))
-                    todo.append(("s", k))
+                if sdone["n"] < len(strig):
+                    trig_s(strig[sdone["n"]][0], strig[sdone["n"]][1])
+                    sdone["n"] += 1
+            quantise(s)
+            if s in SUB_AT:
+                reduce_angles(SUB_AT[s])
+            ready = len(todo) > state["half"]
+            if s >= 2:
+                add_bias(s - 2)
             if ready:
                 next_half()
-            if c + X_BUFS < NG:
-                load(c + X_BUFS)
-        add_bias(NG - 1)
-        todo.append(("p", unit_of[NG - 1]))
-        todo.append(("s", unit_of[NG - 1]))
-        while done["n"] < len(todo):
+            if s >= 1:
+                multiply(s - 1)
+        multiply(ns - 1)
+        ready = len(todo) > state["half"]
+        add_bias(ns - 2)
+        if ready:
+            next_half()
+        add_bias(ns - 1)
+        while state["half"] < len(todo):
             next_half()

@@ -21,17 +21,19 @@ NT = 64
 LT = 4
 NL = NT // LT
 XT_BUFS = 6
-X_BUFS = 10
-TQ = 16
+X_BUFS = 9
+TQ = 32
 HALF = 32
 
 GROUPS = (
     (0, 1), (1, 1), (2, 2), (4, 4), (8, 4), (12, 4), (16, 4), (20, 4), (24, 4), (28, 4), (32, 4),
-    (36, 4), (40, 4), (44, 4), (48, 4), (52, 4), (56, 4), (60, 2), (62, 1), (63, 1),
+    (36, 4), (40, 4), (44, 4), (48, 4), (52, 4), (56, 4), (60, 4),
 )
-UNITS = ((0, 8), (8, 8), (16, 8), (24, 8), (32, 8), (40, 8), (48, 8), (56, 4), (60, 2), (62, 2))
-SUB_AT = {1: 0, 2: 1, 3: 2, 4: 3}
-TRIG_AT = {3: 0, 5: 1, 8: 2, 12: 3}
+UNITS = ((0, 16), (16, 16), (32, 16), (48, 12), (60, 4))
+UT = 16
+SUB_AT = {2: 0, 4: 1}
+TRIG_AT = {4: 0, 7: 1}
+PIECES = 2
 SPLIT_LOADS = (0, NL - 1)
 
 
@@ -41,7 +43,7 @@ def tile_decoder_cross_projector_t_kernel(tc, node, node_mass, W, b, out):
         const = ctx.enter_context(tc.tile_pool(name="const", bufs=1))
         xpool = ctx.enter_context(tc.tile_pool(name="xpool", bufs=X_BUFS))
         gpool = ctx.enter_context(tc.tile_pool(name="gpool", bufs=3))
-        rpool = ctx.enter_context(tc.tile_pool(name="rpool", bufs=4))
+        rpool = ctx.enter_context(tc.tile_pool(name="rpool", bufs=3))
         tpool = ctx.enter_context(tc.tile_pool(name="tpool", bufs=2))
         xtp = ctx.enter_context(tc.psum_pool(name="xtp", bufs=XT_BUFS))
         accp = ctx.enter_context(tc.psum_pool(name="accp", bufs=2))
@@ -89,8 +91,9 @@ def tile_decoder_cross_projector_t_kernel(tc, node, node_mass, W, b, out):
 
         ones = const.tile([P, P], BF16, name="ones")
         nc.vector.memset(ones[:], 1.0)
-        q25 = const.tile([P, 1], F32, name="q25")
-        nc.vector.memset(q25[:], 0.25)
+        hpi = const.tile([P, 1], F32, name="hpi")
+        nc.vector.memset(hpi[:], 1.0)
+        nc.vector.tensor_scalar(out=hpi[:], in0=hpi[:], scalar1=math.pi / 2.0, scalar2=None, op0=ALU.mult)
 
         freq = const.tile([P, HALF], F32, name="freq")
         nc.vector.memset(freq[:, 0:1], 1.0)
@@ -160,14 +163,9 @@ def tile_decoder_cross_projector_t_kernel(tc, node, node_mass, W, b, out):
             elif step == 1:
                 tmp["a"] = tpool.tile([P, TQ, HALF], F32, name="ab", tag="ab")
                 nc.scalar.activation(out=tmp["a"][:], in_=d, func=ACT.Abs)
-            elif step == 2:
-                tmp["z"] = tpool.tile([P, TQ, HALF], F32, name="zz", tag="zz")
-                nc.scalar.activation(
-                    out=tmp["z"][:], in_=tmp["a"][:], func=ACT.Identity, scale=-1.0, bias=q25[:]
-                )
             else:
                 nc.scalar.activation(
-                    out=cs[:, i0 : i0 + TQ, 0, :], in_=tmp["z"][:], func=ACT.Sin, scale=2.0 * math.pi
+                    out=cs[:, i0 : i0 + TQ, 0, :], in_=tmp["a"][:], func=ACT.Sin, scale=-2.0 * math.pi, bias=hpi[:]
                 )
 
         xts = {}
@@ -207,7 +205,7 @@ def tile_decoder_cross_projector_t_kernel(tc, node, node_mass, W, b, out):
             s = group_of[bk]
             il = bk - GROUPS[s][0]
             if il == 0:
-                grp[s] = gpool.tile([P, 4 * K], BF16, name="grouped", tag="grouped", bufs=5, align_bytes=64)
+                grp[s] = gpool.tile([P, 4 * K], BF16, name="grouped", tag="grouped", bufs=4, align_bytes=64)
             dst = grp[s][:].bitcast(F32)[:, il * 512 : (il + 1) * 512].rearrange(
                 "p (g t u) -> p g t u", g=2, u=2
             )
@@ -247,7 +245,7 @@ def tile_decoder_cross_projector_t_kernel(tc, node, node_mass, W, b, out):
             k = unit_of[s]
             u0, un = UNITS[k]
             if t0 == u0:
-                res[k] = rpool.tile([P, 2, 8 * 64], F32, name="res", tag="res")
+                res[k] = rpool.tile([P, 2, UT * 64], F32, name="res", tag="res")
             off = (t0 - u0) * 64
             nc.vector.tensor_tensor(
                 out=res[k][:, :, off : off + nt * 64].rearrange("p g (i d) -> p i g d", d=64),
@@ -256,25 +254,31 @@ def tile_decoder_cross_projector_t_kernel(tc, node, node_mass, W, b, out):
                 op=ALU.add,
             )
             if t0 + nt == u0 + un:
-                todo.append(("p", k))
+                todo.append(("b", k))
+                todo.append(("a", k))
                 todo.append(("s", k))
 
-        def products(k):
+        def sine_products(k):
             i0, nt = UNITS[k]
             xh = res[k][:, 0, 0 : nt * 64].rearrange("p (i h j) -> p i h j", h=2, j=HALF)
-            ta = tpool.tile([P, 8, 2, HALF], F32, name="ta", tag="ta")
-            tb = tpool.tile([P, 8, 2, HALF], F32, name="tb", tag="tb")
-            cosv = cs[:, i0 : i0 + nt, 0:1, :].to_broadcast([P, nt, 2, HALF])
+            tb = tpool.tile([P, UT, 2, HALF], F32, name="tb", tag="tb")
             sinv = cs[:, i0 : i0 + nt, 1, :]
             nc.vector.tensor_tensor(out=tb[:, 0:nt, 0, :], in0=xh[:, :, 1, :], in1=sinv, op=ALU.mult)
             nc.vector.tensor_tensor(out=tb[:, 0:nt, 1, :], in0=xh[:, :, 0, :], in1=sinv, op=ALU.mult)
+            prod[("b", k)] = tb
+
+        def cosine_products(k):
+            i0, nt = UNITS[k]
+            xh = res[k][:, 0, 0 : nt * 64].rearrange("p (i h j) -> p i h j", h=2, j=HALF)
+            ta = tpool.tile([P, UT, 2, HALF], F32, name="ta", tag="ta")
+            cosv = cs[:, i0 : i0 + nt, 0:1, :].to_broadcast([P, nt, 2, HALF])
             nc.vector.tensor_tensor(out=ta[:, 0:nt, :, :], in0=xh, in1=cosv, op=ALU.mult)
-            prod[k] = (ta, tb)
+            prod[("a", k)] = ta
 
         def sums_and_store(k):
             i0, nt = UNITS[k]
             xh = res[k][:, 0, 0 : nt * 64].rearrange("p (i h j) -> p i h j", h=2, j=HALF)
-            ta, tb = prod[k]
+            ta, tb = prod[("a", k)], prod[("b", k)]
             nc.vector.tensor_tensor(
                 out=xh[:, :, 0, :], in0=ta[:, 0:nt, 0, :], in1=tb[:, 0:nt, 0, :], op=ALU.subtract
             )
@@ -284,8 +288,10 @@ def tile_decoder_cross_projector_t_kernel(tc, node, node_mass, W, b, out):
         def next_half():
             kind, k = todo[state["half"]]
             state["half"] += 1
-            if kind == "p":
-                products(k)
+            if kind == "b":
+                sine_products(k)
+            elif kind == "a":
+                cosine_products(k)
             else:
                 sums_and_store(k)
 
@@ -296,7 +302,7 @@ def tile_decoder_cross_projector_t_kernel(tc, node, node_mass, W, b, out):
         for s in range(ns):
             t0, nt = GROUPS[s]
             if s in TRIG_AT:
-                for step in range(4):
+                for step in range(3):
                     strig.append((TRIG_AT[s], step))
             for bk in range(t0, t0 + nt):
                 copy_out(bk)
@@ -307,17 +313,16 @@ def tile_decoder_cross_projector_t_kernel(tc, node, node_mass, W, b, out):
             quantise(s)
             if s in SUB_AT:
                 reduce_angles(SUB_AT[s])
-            ready = len(todo) > state["half"]
+            ready = min(PIECES, len(todo) - state["half"])
             if s >= 2:
                 add_bias(s - 2)
-            if ready:
+            for r in range(ready):
                 next_half()
             if s >= 1:
                 multiply(s - 1)
         multiply(ns - 1)
-        ready = len(todo) > state["half"]
         add_bias(ns - 2)
-        if ready:
+        for r in range(min(PIECES, len(todo) - state["half"])):
             next_half()
         add_bias(ns - 1)
         while state["half"] < len(todo):

@@ -21,19 +21,19 @@ NT = 64
 LT = 4
 NL = NT // LT
 XT_BUFS = 6
-X_BUFS = 9
+X_BUFS = 10
 TQ = 32
 HALF = 32
 
 GROUPS = (
     (0, 1), (1, 1), (2, 2), (4, 4), (8, 4), (12, 4), (16, 4), (20, 4), (24, 4), (28, 4), (32, 4),
-    (36, 4), (40, 4), (44, 4), (48, 4), (52, 4), (56, 4), (60, 4),
+    (36, 4), (40, 4), (44, 4), (48, 4), (52, 4), (56, 4), (60, 2), (62, 1), (63, 1),
 )
-UNITS = ((0, 16), (16, 16), (32, 16), (48, 12), (60, 4))
-UT = 16
+UNITS = ((0, 8), (8, 8), (16, 8), (24, 8), (32, 8), (40, 8), (48, 8), (56, 4), (60, 2), (62, 2))
 SUB_AT = {2: 0, 4: 1}
 TRIG_AT = {4: 0, 7: 1}
-PIECES = 2
+G_UNITS = (0, 1, 2, 4)
+V_FIRST = (8, 13)
 SPLIT_LOADS = (0, NL - 1)
 
 
@@ -43,7 +43,7 @@ def tile_decoder_cross_projector_t_kernel(tc, node, node_mass, W, b, out):
         const = ctx.enter_context(tc.tile_pool(name="const", bufs=1))
         xpool = ctx.enter_context(tc.tile_pool(name="xpool", bufs=X_BUFS))
         gpool = ctx.enter_context(tc.tile_pool(name="gpool", bufs=3))
-        rpool = ctx.enter_context(tc.tile_pool(name="rpool", bufs=3))
+        rpool = ctx.enter_context(tc.tile_pool(name="rpool", bufs=5))
         tpool = ctx.enter_context(tc.tile_pool(name="tpool", bufs=2))
         xtp = ctx.enter_context(tc.psum_pool(name="xtp", bufs=XT_BUFS))
         accp = ctx.enter_context(tc.psum_pool(name="accp", bufs=2))
@@ -201,15 +201,19 @@ def tile_decoder_cross_projector_t_kernel(tc, node, node_mass, W, b, out):
                 if il == LT - 1 and bk // LT + X_BUFS < NL:
                     load(bk // LT + X_BUFS)
 
-        def copy_out(bk):
+        def copy_out(bk, on_vector):
             s = group_of[bk]
             il = bk - GROUPS[s][0]
             if il == 0:
-                grp[s] = gpool.tile([P, 4 * K], BF16, name="grouped", tag="grouped", bufs=4, align_bytes=64)
+                grp[s] = gpool.tile([P, 4 * K], BF16, name="grouped", tag="grouped", bufs=5, align_bytes=64)
             dst = grp[s][:].bitcast(F32)[:, il * 512 : (il + 1) * 512].rearrange(
                 "p (g t u) -> p g t u", g=2, u=2
             )
-            nc.scalar.copy(out=dst, in_=xts[bk][:].rearrange("p (g u t) -> p g t u", g=2, u=2))
+            src = xts[bk][:].rearrange("p (g u t) -> p g t u", g=2, u=2)
+            if on_vector:
+                nc.vector.tensor_copy(out=dst, in_=src)
+            else:
+                nc.scalar.copy(out=dst, in_=src)
 
         def quantise(s):
             nt = GROUPS[s][1]
@@ -245,7 +249,7 @@ def tile_decoder_cross_projector_t_kernel(tc, node, node_mass, W, b, out):
             k = unit_of[s]
             u0, un = UNITS[k]
             if t0 == u0:
-                res[k] = rpool.tile([P, 2, UT * 64], F32, name="res", tag="res")
+                res[k] = rpool.tile([P, 2, 8 * 64], F32, name="res", tag="res")
             off = (t0 - u0) * 64
             nc.vector.tensor_tensor(
                 out=res[k][:, :, off : off + nt * 64].rearrange("p g (i d) -> p i g d", d=64),
@@ -254,31 +258,50 @@ def tile_decoder_cross_projector_t_kernel(tc, node, node_mass, W, b, out):
                 op=ALU.add,
             )
             if t0 + nt == u0 + un:
-                todo.append(("b", k))
-                todo.append(("a", k))
-                todo.append(("s", k))
+                if k in G_UNITS:
+                    rotate_on_gpsimd(k)
+                else:
+                    todo.append(("p", k))
+                    todo.append(("s", k))
 
-        def sine_products(k):
+        def rotate_on_gpsimd(k):
             i0, nt = UNITS[k]
             xh = res[k][:, 0, 0 : nt * 64].rearrange("p (i h j) -> p i h j", h=2, j=HALF)
-            tb = tpool.tile([P, UT, 2, HALF], F32, name="tb", tag="tb")
+            ga = tpool.tile([P, 8, 2, HALF], F32, name="ga", tag="ga")
+            gb = tpool.tile([P, 8, 2, HALF], F32, name="gb", tag="gb")
+            sinv = cs[:, i0 : i0 + nt, 1, :]
+            hn = nt // 2
+            nc.gpsimd.tensor_tensor(out=gb[:, 0:nt, 0, :], in0=xh[:, :, 1, :], in1=sinv, op=ALU.mult)
+            nc.gpsimd.tensor_tensor(out=gb[:, 0:nt, 1, :], in0=xh[:, :, 0, :], in1=sinv, op=ALU.mult)
+            for a in (0, hn):
+                nc.gpsimd.tensor_tensor(
+                    out=ga[:, a : a + hn, :, :],
+                    in0=xh[:, a : a + hn, :, :],
+                    in1=cs[:, i0 + a : i0 + a + hn, 0:1, :].to_broadcast([P, hn, 2, HALF]),
+                    op=ALU.mult,
+                )
+            nc.gpsimd.tensor_tensor(
+                out=xh[:, :, 0, :], in0=ga[:, 0:nt, 0, :], in1=gb[:, 0:nt, 0, :], op=ALU.subtract
+            )
+            nc.gpsimd.tensor_tensor(out=xh[:, :, 1, :], in0=ga[:, 0:nt, 1, :], in1=gb[:, 0:nt, 1, :], op=ALU.add)
+            nc.sync.dma_start(out=out_v[:, :, i0 * 64 : (i0 + nt) * 64], in_=res[k][:, :, 0 : nt * 64])
+
+        def products(k):
+            i0, nt = UNITS[k]
+            xh = res[k][:, 0, 0 : nt * 64].rearrange("p (i h j) -> p i h j", h=2, j=HALF)
+            ta = tpool.tile([P, 8, 2, HALF], F32, name="ta", tag="ta")
+            tb = tpool.tile([P, 8, 2, HALF], F32, name="tb", tag="tb")
+            cosv = cs[:, i0 : i0 + nt, 0:1, :].to_broadcast([P, nt, 2, HALF])
             sinv = cs[:, i0 : i0 + nt, 1, :]
             nc.vector.tensor_tensor(out=tb[:, 0:nt, 0, :], in0=xh[:, :, 1, :], in1=sinv, op=ALU.mult)
             nc.vector.tensor_tensor(out=tb[:, 0:nt, 1, :], in0=xh[:, :, 0, :], in1=sinv, op=ALU.mult)
-            prod[("b", k)] = tb
-
-        def cosine_products(k):
-            i0, nt = UNITS[k]
-            xh = res[k][:, 0, 0 : nt * 64].rearrange("p (i h j) -> p i h j", h=2, j=HALF)
-            ta = tpool.tile([P, UT, 2, HALF], F32, name="ta", tag="ta")
-            cosv = cs[:, i0 : i0 + nt, 0:1, :].to_broadcast([P, nt, 2, HALF])
             nc.vector.tensor_tensor(out=ta[:, 0:nt, :, :], in0=xh, in1=cosv, op=ALU.mult)
-            prod[("a", k)] = ta
+            prod[k] = (ta, tb)
 
         def sums_and_store(k):
             i0, nt = UNITS[k]
             xh = res[k][:, 0, 0 : nt * 64].rearrange("p (i h j) -> p i h j", h=2, j=HALF)
-            ta, tb = prod[("a", k)], prod[("b", k)]
+            ta, tb = prod[k]
             nc.vector.tensor_tensor(
                 out=xh[:, :, 0, :], in0=ta[:, 0:nt, 0, :], in1=tb[:, 0:nt, 0, :], op=ALU.subtract
             )
@@ -288,10 +311,8 @@ def tile_decoder_cross_projector_t_kernel(tc, node, node_mass, W, b, out):
         def next_half():
             kind, k = todo[state["half"]]
             state["half"] += 1
-            if kind == "b":
-                sine_products(k)
-            elif kind == "a":
-                cosine_products(k)
+            if kind == "p":
+                products(k)
             else:
                 sums_and_store(k)
 
@@ -305,24 +326,30 @@ def tile_decoder_cross_projector_t_kernel(tc, node, node_mass, W, b, out):
                 for step in range(3):
                     strig.append((TRIG_AT[s], step))
             for bk in range(t0, t0 + nt):
-                copy_out(bk)
+                if bk == t0 and s in V_FIRST:
+                    continue
+                copy_out(bk, False)
                 transposes_upto(bk + XT_BUFS + 1)
                 if sdone["n"] < len(strig):
                     trig_s(strig[sdone["n"]][0], strig[sdone["n"]][1])
                     sdone["n"] += 1
             quantise(s)
+            if s + 1 in V_FIRST:
+                copy_out(GROUPS[s + 1][0], True)
+                transposes_upto(GROUPS[s + 1][0] + XT_BUFS + 1)
             if s in SUB_AT:
                 reduce_angles(SUB_AT[s])
-            ready = min(PIECES, len(todo) - state["half"])
+            ready = len(todo) > state["half"]
             if s >= 2:
                 add_bias(s - 2)
-            for r in range(ready):
+            if ready:
                 next_half()
             if s >= 1:
                 multiply(s - 1)
         multiply(ns - 1)
+        ready = len(todo) > state["half"]
         add_bias(ns - 2)
-        for r in range(min(PIECES, len(todo) - state["half"])):
+        if ready:
             next_half()
         add_bias(ns - 1)
         while state["half"] < len(todo):

@@ -26,15 +26,15 @@ TQ = 32
 HALF = 32
 
 GROUPS = (
-    (0, 1), (1, 1), (2, 2), (4, 4), (8, 4), (12, 4), (16, 4), (20, 4), (24, 4), (28, 4), (32, 4),
+    (0, 1), (1, 1), (2, 2), (4, 2), (6, 2), (8, 4), (12, 4), (16, 4), (20, 4), (24, 4), (28, 4), (32, 4),
     (36, 4), (40, 4), (44, 4), (48, 4), (52, 4), (56, 4), (60, 2), (62, 1), (63, 1),
 )
 UNITS = ((0, 8), (8, 8), (16, 8), (24, 8), (32, 8), (40, 8), (48, 8), (56, 4), (60, 2), (62, 2))
-SUB_AT = {2: 0, 4: 1}
-TRIG_AT = {4: 0, 7: 1}
-G_UNITS = (0, 1, 2, 4)
-V_FIRST = (8, 13)
-SPLIT_LOADS = (0, NL - 1)
+SUB_AT = {4: 0, 6: 1}
+TRIG_AT = {6: 0, 9: 1}
+G_UNITS = ()
+V_FIRST = ()
+SPLIT_LOADS = (0, 1, NL - 1)
 
 
 def tile_decoder_cross_projector_t_kernel(tc, node, node_mass, W, b, out):

import math
from contextlib import ExitStack

import concourse.mybir as mybir
from concourse.masks import make_identity

FLOPS = 2 * 8192 * 1024 * 128

F32 = mybir.dt.float32
BF16 = mybir.dt.bfloat16
I32 = mybir.dt.int32
U32 = mybir.dt.uint32
U8 = mybir.dt.uint8
FP8X4 = mybir.dt.float8_e4m3fn_x4
ALU = mybir.AluOpType
ACT = mybir.ActivationFunctionType

P = 128
K = 1024
NT = 64
LT = 4
NL = NT // LT
XT_BUFS = 6
X_BUFS = 10
TQ = 32
HALF = 32

GROUPS = (
    (0, 1), (1, 1), (2, 2), (4, 2), (6, 2), (8, 4), (12, 4), (16, 4), (20, 4), (24, 4), (28, 4), (32, 4),
    (36, 4), (40, 4), (44, 4), (48, 4), (52, 4), (56, 4), (60, 2), (62, 1), (63, 1),
)
UNITS = ((0, 8), (8, 8), (16, 8), (24, 8), (32, 8), (40, 8), (48, 8), (56, 4), (60, 2), (62, 2))
SUB_AT = {4: 0, 6: 1}
TRIG_AT = {6: 0, 9: 1}
G_UNITS = ()
V_FIRST = ()
SPLIT_LOADS = (0, 1, NL - 1)


def tile_decoder_cross_projector_t_kernel(tc, node, node_mass, W, b, out):
    nc = tc.nc
    with ExitStack() as ctx:
        const = ctx.enter_context(tc.tile_pool(name="const", bufs=1))
        xpool = ctx.enter_context(tc.tile_pool(name="xpool", bufs=X_BUFS))
        gpool = ctx.enter_context(tc.tile_pool(name="gpool", bufs=3))
        rpool = ctx.enter_context(tc.tile_pool(name="rpool", bufs=5))
        tpool = ctx.enter_context(tc.tile_pool(name="tpool", bufs=2))
        xtp = ctx.enter_context(tc.psum_pool(name="xtp", bufs=XT_BUFS))
        accp = ctx.enter_context(tc.psum_pool(name="accp", bufs=2))
        ctx.enter_context(tc.manual_schedule())

        node_v = node.rearrange("b (q i) k -> (b q) (i k)", i=NT)
        mass_v = node_mass.rearrange("b (q i) -> (b q) i", i=NT)
        out_v = out.rearrange("g b o (q i) d -> (b o q) g (i d)", i=NT)

        mass_bf = const.tile([P, NT], BF16, name="mass_bf")
        nc.scalar.dma_start(out=mass_bf[:], in_=mass_v)
        wraw = const.tile([P, 1024], BF16, name="wraw")
        nc.scalar.dma_start(
            out=wraw[:].rearrange("p (c x) -> p c x", c=4),
            in_=W.rearrange("(c p e) n -> p c (e n)", c=4, p=P, e=2),
        )
        brow = const.tile([P, P], BF16, name="brow")
        nc.vector.memset(brow[:], 0.0)
        nc.scalar.dma_start(out=brow[0:1, :], in_=b.rearrange("(o n) -> o n", o=1))

        xs = {}

        def load(l):
            x = xpool.tile([P, LT * K], BF16, name="x", tag="x")
            xs[l] = x
            if l in SPLIT_LOADS:
                for il in range(LT):
                    nc.sync.dma_start(
                        out=x[:, il * K : (il + 1) * K],
                        in_=node_v[:, (l * LT + il) * K : (l * LT + il + 1) * K],
                    )
            else:
                nc.sync.dma_start(out=x[:], in_=node_v[:, l * LT * K : (l + 1) * LT * K])

        for l in range(X_BUFS):
            load(l)

        zero1 = const.tile([P, 1], F32, name="zero1")
        nc.vector.memset(zero1[:], 0.0)
        warm = const.tile([P, 1], F32, name="warm")
        nc.scalar.activation(out=warm[:], in_=zero1[:], func=ACT.Sin)

        ident = const.tile([P, P], F32, name="ident")
        make_identity(nc, ident[:])

        ones = const.tile([P, P], BF16, name="ones")
        nc.vector.memset(ones[:], 1.0)
        hpi = const.tile([P, 1], F32, name="hpi")
        nc.vector.memset(hpi[:], 1.0)
        nc.vector.tensor_scalar(out=hpi[:], in0=hpi[:], scalar1=math.pi / 2.0, scalar2=None, op0=ALU.mult)

        freq = const.tile([P, HALF], F32, name="freq")
        nc.vector.memset(freq[:, 0:1], 1.0)
        nc.vector.tensor_scalar(
            out=freq[:, 0:1], in0=freq[:, 0:1], scalar1=1.0 / (2.0 * math.pi), scalar2=None, op0=ALU.mult
        )
        ratio = 10000.0 ** (-1.0 / HALF)
        w = 1
        while w < HALF:
            nc.vector.tensor_scalar(
                out=freq[:, w : 2 * w], in0=freq[:, 0:w], scalar1=ratio**w, scalar2=None, op0=ALU.mult
            )
            w *= 2

        massf = const.tile([P, NT], F32, name="massf")
        nc.gpsimd.tensor_copy(out=massf[:], in_=mass_bf[:])
        turns = const.tile([P, NT, HALF], F32, name="turns")
        whole = const.tile([P, NT, HALF], I32, name="whole")
        for q in range(NT // TQ):
            i0 = q * TQ
            nc.gpsimd.tensor_tensor(
                out=turns[:, i0 : i0 + TQ, :],
                in0=massf[:, i0 : i0 + TQ].unsqueeze(2).to_broadcast([P, TQ, HALF]),
                in1=freq[:].unsqueeze(1).to_broadcast([P, TQ, HALF]),
                op=ALU.mult,
            )
            nc.gpsimd.tensor_scalar(
                out=whole[:, i0 : i0 + TQ, :],
                in0=turns[:, i0 : i0 + TQ, :],
                scalar1=1.0,
                scalar2=0.0,
                op0=ALU.mult,
                op1=ALU.add,
            )

        def reduce_angles(q):
            i0 = q * TQ
            nc.vector.tensor_tensor(
                out=turns[:, i0 : i0 + TQ, :],
                in0=turns[:, i0 : i0 + TQ, :],
                in1=whole[:, i0 : i0 + TQ, :],
                op=ALU.subtract,
            )

        wgrp = const.tile([P, 1024], BF16, name="wgrp", align_bytes=64)
        nc.vector.tensor_copy(
            out=wgrp[:].rearrange("p (g n t) -> p g n t", g=2, t=4),
            in_=wraw[:].rearrange("p (g t n) -> p g n t", g=2, t=4),
        )
        wcodes = const.tile([P, 256], U32, name="wcodes", align_bytes=64)
        wsc = const.tile([P, 256], U8, name="wsc", align_bytes=64)
        nc.vector.quantize_mx(out=wcodes[:].bitcast(FP8X4), scales=wsc[:], in_=wgrp[:])

        bps = accp.tile([P, 512], F32, name="bps", tag="acc")
        nc.tensor.matmul(out=bps[:, 0:P], lhsT=ones[:], rhs=brow[:], start=True, stop=True)
        bias = const.tile([P, P], F32, name="bias")
        nc.scalar.copy(out=bias[:], in_=bps[:, 0:P])

        cs = const.tile([P, NT, 2, HALF], F32, name="cs")
        tmp = {}

        def trig_s(q, step):
            i0 = q * TQ
            d = turns[:, i0 : i0 + TQ, :]
            if step == 0:
                nc.scalar.activation(out=cs[:, i0 : i0 + TQ, 1, :], in_=d, func=ACT.Sin, scale=2.0 * math.pi)
            elif step == 1:
                tmp["a"] = tpool.tile([P, TQ, HALF], F32, name="ab", tag="ab")
                nc.scalar.activation(out=tmp["a"][:], in_=d, func=ACT.Abs)
            else:
                nc.scalar.activation(
                    out=cs[:, i0 : i0 + TQ, 0, :], in_=tmp["a"][:], func=ACT.Sin, scale=-2.0 * math.pi, bias=hpi[:]
                )

        xts = {}
        state = {"tb": 0, "half": 0}
        grp = {}
        qnt = {}
        accs = {}
        res = {}
        prod = {}
        group_of = {}
        for s, (t0, nt) in enumerate(GROUPS):
            for t in range(t0, t0 + nt):
                group_of[t] = s
        unit_of = {}
        for k, (t0, nt) in enumerate(UNITS):
            for t in range(t0, t0 + nt):
                unit_of[group_of[t]] = k

        def transposes_upto(n):
            while state["tb"] < min(n, NT):
                bk = state["tb"]
                xf = xs[bk // LT][:].bitcast(F32)
                il = bk % LT
                xt = xtp.tile([P, 512], F32, name="xt", tag="xt")
                for wb in range(4):
                    nc.tensor.transpose(
                        xt[:, wb * P : (wb + 1) * P],
                        xf[:, il * 512 + wb * P : il * 512 + (wb + 1) * P],
                        ident[:],
                    )
                xts[bk] = xt
                state["tb"] = bk + 1
                if il == LT - 1 and bk // LT + X_BUFS < NL:
                    load(bk // LT + X_BUFS)

        def copy_out(bk, on_vector):
            s = group_of[bk]
            il = bk - GROUPS[s][0]
            if il == 0:
                grp[s] = gpool.tile([P, 4 * K], BF16, name="grouped", tag="grouped", bufs=5, align_bytes=64)
            dst = grp[s][:].bitcast(F32)[:, il * 512 : (il + 1) * 512].rearrange(
                "p (g t u) -> p g t u", g=2, u=2
            )
            src = xts[bk][:].rearrange("p (g u t) -> p g t u", g=2, u=2)
            if on_vector:
                nc.vector.tensor_copy(out=dst, in_=src)
            else:
                nc.scalar.copy(out=dst, in_=src)

        def quantise(s):
            nt = GROUPS[s][1]
            codes = gpool.tile([P, 4 * 256], U32, name="codes", tag="codes", align_bytes=64)
            sc = gpool.tile([P, 4 * 256], U8, name="sc", tag="sc", align_bytes=64)
            nc.vector.quantize_mx(
                out=codes[:, 0 : nt * 256].bitcast(FP8X4), scales=sc[:, 0 : nt * 256], in_=grp[s][:, 0 : nt * K]
            )
            qnt[s] = (codes, sc)

        def multiply(s):
            nt = GROUPS[s][1]
            codes, sc = qnt[s]
            acc = accp.tile([P, 512], F32, name="acc", tag="acc")
            for il in range(nt):
                for g in range(2):
                    o = (il * 2 + g) * P
                    nc.tensor.matmul_mx(
                        out=acc[:, il * P : (il + 1) * P],
                        lhsT=codes[:, o : o + P].bitcast(FP8X4),
                        lhsT_scale=sc[:, o : o + P],
                        rhs=wcodes[:, g * P : (g + 1) * P].bitcast(FP8X4),
                        rhs_scale=wsc[:, g * P : (g + 1) * P],
                        start=(g == 0),
                        stop=(g == 1),
                    )
            accs[s] = acc

        todo = []

        def add_bias(s):
            t0, nt = GROUPS[s]
            k = unit_of[s]
            u0, un = UNITS[k]
            if t0 == u0:
                res[k] = rpool.tile([P, 2, 8 * 64], F32, name="res", tag="res")
            off = (t0 - u0) * 64
            nc.vector.tensor_tensor(
                out=res[k][:, :, off : off + nt * 64].rearrange("p g (i d) -> p i g d", d=64),
                in0=accs[s][:, 0 : nt * P].rearrange("p (i g d) -> p i g d", i=nt, g=2),
                in1=bias[:].rearrange("p (g d) -> p g d", g=2).unsqueeze(1).to_broadcast([P, nt, 2, 64]),
                op=ALU.add,
            )
            if t0 + nt == u0 + un:
                if k in G_UNITS:
                    rotate_on_gpsimd(k)
                else:
                    todo.append(("p", k))
                    todo.append(("s", k))

        def rotate_on_gpsimd(k):
            i0, nt = UNITS[k]
            xh = res[k][:, 0, 0 : nt * 64].rearrange("p (i h j) -> p i h j", h=2, j=HALF)
            ga = tpool.tile([P, 8, 2, HALF], F32, name="ga", tag="ga")
            gb = tpool.tile([P, 8, 2, HALF], F32, name="gb", tag="gb")
            sinv = cs[:, i0 : i0 + nt, 1, :]
            hn = nt // 2
            nc.gpsimd.tensor_tensor(out=gb[:, 0:nt, 0, :], in0=xh[:, :, 1, :], in1=sinv, op=ALU.mult)
            nc.gpsimd.tensor_tensor(out=gb[:, 0:nt, 1, :], in0=xh[:, :, 0, :], in1=sinv, op=ALU.mult)
            for a in (0, hn):
                nc.gpsimd.tensor_tensor(
                    out=ga[:, a : a + hn, :, :],
                    in0=xh[:, a : a + hn, :, :],
                    in1=cs[:, i0 + a : i0 + a + hn, 0:1, :].to_broadcast([P, hn, 2, HALF]),
                    op=ALU.mult,
                )
            nc.gpsimd.tensor_tensor(
                out=xh[:, :, 0, :], in0=ga[:, 0:nt, 0, :], in1=gb[:, 0:nt, 0, :], op=ALU.subtract
            )
            nc.gpsimd.tensor_tensor(out=xh[:, :, 1, :], in0=ga[:, 0:nt, 1, :], in1=gb[:, 0:nt, 1, :], op=ALU.add)
            nc.sync.dma_start(out=out_v[:, :, i0 * 64 : (i0 + nt) * 64], in_=res[k][:, :, 0 : nt * 64])

        def products(k):
            i0, nt = UNITS[k]
            xh = res[k][:, 0, 0 : nt * 64].rearrange("p (i h j) -> p i h j", h=2, j=HALF)
            ta = tpool.tile([P, 8, 2, HALF], F32, name="ta", tag="ta")
            tb = tpool.tile([P, 8, 2, HALF], F32, name="tb", tag="tb")
            cosv = cs[:, i0 : i0 + nt, 0:1, :].to_broadcast([P, nt, 2, HALF])
            sinv = cs[:, i0 : i0 + nt, 1, :]
            nc.vector.tensor_tensor(out=tb[:, 0:nt, 0, :], in0=xh[:, :, 1, :], in1=sinv, op=ALU.mult)
            nc.vector.tensor_tensor(out=tb[:, 0:nt, 1, :], in0=xh[:, :, 0, :], in1=sinv, op=ALU.mult)
            nc.vector.tensor_tensor(out=ta[:, 0:nt, :, :], in0=xh, in1=cosv, op=ALU.mult)
            prod[k] = (ta, tb)

        def sums_and_store(k):
            i0, nt = UNITS[k]
            xh = res[k][:, 0, 0 : nt * 64].rearrange("p (i h j) -> p i h j", h=2, j=HALF)
            ta, tb = prod[k]
            nc.vector.tensor_tensor(
                out=xh[:, :, 0, :], in0=ta[:, 0:nt, 0, :], in1=tb[:, 0:nt, 0, :], op=ALU.subtract
            )
            nc.vector.tensor_tensor(out=xh[:, :, 1, :], in0=ta[:, 0:nt, 1, :], in1=tb[:, 0:nt, 1, :], op=ALU.add)
            nc.sync.dma_start(out=out_v[:, :, i0 * 64 : (i0 + nt) * 64], in_=res[k][:, :, 0 : nt * 64])

        def next_half():
            kind, k = todo[state["half"]]
            state["half"] += 1
            if kind == "p":
                products(k)
            else:
                sums_and_store(k)

        ns = len(GROUPS)
        strig = []
        sdone = {"n": 0}
        transposes_upto(XT_BUFS)
        for s in range(ns):
            t0, nt = GROUPS[s]
            if s in TRIG_AT:
                for step in range(3):
                    strig.append((TRIG_AT[s], step))
            for bk in range(t0, t0 + nt):
                if bk == t0 and s in V_FIRST:
                    continue
                copy_out(bk, False)
                transposes_upto(bk + XT_BUFS + 1)
                if sdone["n"] < len(strig):
                    trig_s(strig[sdone["n"]][0], strig[sdone["n"]][1])
                    sdone["n"] += 1
            quantise(s)
            if s + 1 in V_FIRST:
                copy_out(GROUPS[s + 1][0], True)
                transposes_upto(GROUPS[s + 1][0] + XT_BUFS + 1)
            if s in SUB_AT:
                reduce_angles(SUB_AT[s])
            ready = len(todo) > state["half"]
            if s >= 2:
                add_bias(s - 2)
            if ready:
                next_half()
            if s >= 1:
                multiply(s - 1)
        multiply(ns - 1)
        ready = len(todo) > state["half"]
        add_bias(ns - 2)
        if ready:
            next_half()
        add_bias(ns - 1)
        while state["half"] < len(todo):
            next_half()
